import numpy as np
import ml_dtypes

BF16 = ml_dtypes.bfloat16


def bf(x):
    return np.asarray(x, np.float32).astype(BF16)


def f32(x):
    return np.asarray(x, np.float32)


def f64(x):
    return np.asarray(x).astype(np.float64)


def striped(idx):
    return np.tile(idx.reshape(-1, 16).T, (8, 1))


L, B, C, S, K, KK, T, OUT, PER, N = 2, 128, 256, 2048, 4, 16, 256, 16, 16, 1024
ARS = (np.arange(L) + 1.0)[::-1]
MEANS = f32(ARS / ARS.sum())


def residual_levels(x):
    resid, outs = x, []
    for l in range(L):
        o = MEANS[l] * np.where(resid >= 0.0, np.float32(1.0), np.float32(-1.0))
        outs.append(o)
        resid = resid - o
    return np.stack(outs)


def setup_inputs():
    q = f32(residual_levels(f32(np.random.standard_normal((B, S)))).reshape(C, S))
    w = f32(0.5 * np.random.standard_normal((KK, T)))
    bias = f32(0.1 * np.random.standard_normal((1, OUT)))
    return {"q": q, "w": w, "bias": bias, "offs": striped(np.random.permutation(np.tile(np.arange(S), 2))[:N])}


def reference(q, w, bias, offs):
    idx = offs[:16].T.reshape(-1)
    a = f64(q)[:, idx].reshape(C, K, T)
    u = np.broadcast_to(f64(w)[None], (C, KK, T))
    for i in range(K):
        lo, hi = u[:, 0::2], u[:, 1::2]
        u = 0.5 * (lo + hi) + a[:, i, None, :] * (0.5 * (hi - lo))
    lut = u[:, 0].reshape(L, B, T).sum(axis=0)
    return lut.reshape(B, OUT, PER).sum(axis=-1) + f64(bias)

@@ -1,0 +1,87 @@
+import concourse.mybir as mybir
+
+F32 = mybir.dt.float32
+I32 = mybir.dt.int32
+U16 = mybir.dt.uint16
+ALU = mybir.AluOpType
+
+P = 128
+LEVELS = 2
+S = 2048
+T = 256
+K = 4
+CODES = 16
+OUT = 16
+PER = 16
+N = K * T
+
+FLOPS = 2 * (CODES - 1) * LEVELS * P * T
+
+
+def tile_linearlut_kernel(tc, q, w, bias, offs, out):
+    nc = tc.nc
+    with (
+        tc.tile_pool(name="held", bufs=1) as held,
+        tc.psum_pool(name="psum", bufs=4) as psum,
+    ):
+        offsets = held.tile([P, N // 16], U16, name="offsets")
+        nc.sync.dma_start(offsets[:], offs)
+        window = []
+        for l in range(LEVELS):
+            q_l = held.tile([P, S], F32, name=f"q{l}")
+            nc.sync.dma_start(q_l[:], q[l * P : (l + 1) * P, :])
+            window.append(q_l)
+        w_pad = held.tile([P, T], F32, name="w_pad")
+        nc.gpsimd.memset(w_pad[:], 0.0)
+        nc.scalar.dma_start(w_pad[0:CODES, :], w)
+        bias_all = held.tile([P, OUT], F32, name="bias_all")
+        nc.scalar.dma_start(bias_all[:], bias.to_broadcast([P, OUT]))
+
+        part = held.tile([P, 1], I32, name="part")
+        nc.gpsimd.iota(part[:], pattern=[[0, 1]], base=0, channel_multiplier=1)
+        bit = held.tile([P, K], I32, name="bit")
+        for i in range(K):
+            nc.vector.tensor_scalar(
+                out=bit[:, i : i + 1], in0=part[:], scalar1=i, scalar2=1,
+                op0=ALU.logical_shift_right, op1=ALU.bitwise_and,
+            )
+        sgn = held.tile([P, K], F32, name="sgn")
+        nc.vector.tensor_scalar(out=sgn[:], in0=bit[:], scalar1=2.0, scalar2=-1.0, op0=ALU.mult, op1=ALU.add)
+
+        spread = held.tile([P, CODES, P], F32, name="spread")
+        nc.vector.memset(spread[:, 0, :], 0.0)
+        nc.vector.memset(spread[0:CODES, 0, :], 1.0 / CODES)
+        for i in range(K):
+            n = 1 << i
+            nc.vector.tensor_scalar(
+                out=spread[:, n : 2 * n, :], in0=spread[:, 0:n, :], scalar1=sgn[:, i : i + 1], scalar2=None,
+                op0=ALU.mult,
+            )
+
+        coef = held.tile([P, CODES, T], F32, name="coef")
+        for m in range(0, CODES, 2):
+            bank = psum.tile([P, 2, T], F32, name="bank")
+            for j in range(2):
+                nc.tensor.matmul(bank[:, j, :], spread[:, m + j, :], w_pad[:], start=True, stop=True)
+            nc.scalar.copy(coef[:, m : m + 2, :], bank[:])
+
+        value = [coef for l in range(LEVELS)]
+        for i in range(K):
+            n = CODES >> (i + 1)
+            picks = offsets[:, i * (T // 16) : (i + 1) * (T // 16)]
+            for l in range(LEVELS):
+                pairs = value[l][:].rearrange("p (e two) t -> p e two t", two=2)
+                after = held.tile([P, n, T], F32, name=f"u{i + 1}_{l}")
+                for e in range(n):
+                    nc.vector.tensor_tensor(after[:, e, :], window[l][:].indirect(picks), pairs[:, e, 1, :], ALU.mult)
+                nc.vector.tensor_tensor(after[:], after[:], pairs[:, :, 0, :], ALU.add)
+                value[l] = after
+
+        both = held.tile([P, T], F32, name="both")
+        nc.vector.tensor_tensor(both[:], value[0][:, 0, :], value[1][:, 0, :], ALU.add)
+        sums = held.tile([P, OUT], F32, name="sums")
+        nc.vector.tensor_reduce(
+            out=sums[:], in_=both[:].rearrange("p (o s) -> p o s", s=PER), axis=mybir.AxisListType.X, op=ALU.add
+        )
+        nc.vector.tensor_tensor(sums[:], sums[:], bias_all[:], ALU.add)
+        nc.sync.dma_start(out, sums[:])

@@ -1,4 +1,5 @@
 import concourse.mybir as mybir
+from concourse.masks import make_identity
 
 F32 = mybir.dt.float32
 I32 = mybir.dt.int32
@@ -18,12 +19,22 @@ N = K * T
 FLOPS = 2 * (CODES - 1) * LEVELS * P * T
 
 
+def odd_first(n):
+    return list(range(1, n, 2)) + list(range(0, n, 2))
+
+
 def tile_linearlut_kernel(tc, q, w, bias, offs, out):
     nc = tc.nc
     with (
         tc.tile_pool(name="held", bufs=1) as held,
-        tc.psum_pool(name="psum", bufs=4) as psum,
+        tc.psum_pool(name="psum", bufs=6) as psum,
+        tc.psum_pool(name="psum_total", bufs=1) as psum_total,
     ):
+        w_pad = held.tile([P, T], F32, name="w_pad")
+        for rep in range(2):
+            nc.scalar.dma_start(w_pad[rep * CODES : (rep + 1) * CODES, :], w)
+        nc.any.memset(w_pad[32:64, :], 0.0)
+        nc.any.memset(w_pad[64:128, :], 0.0)
         offsets = held.tile([P, N // 16], U16, name="offsets")
         nc.sync.dma_start(offsets[:], offs)
         window = []
@@ -31,9 +42,6 @@ def tile_linearlut_kernel(tc, q, w, bias, offs, out):
             q_l = held.tile([P, S], F32, name=f"q{l}")
             nc.sync.dma_start(q_l[:], q[l * P : (l + 1) * P, :])
             window.append(q_l)
-        w_pad = held.tile([P, T], F32, name="w_pad")
-        nc.gpsimd.memset(w_pad[:], 0.0)
-        nc.scalar.dma_start(w_pad[0:CODES, :], w)
         bias_all = held.tile([P, OUT], F32, name="bias_all")
         nc.scalar.dma_start(bias_all[:], bias.to_broadcast([P, OUT]))
 
@@ -47,38 +55,52 @@ def tile_linearlut_kernel(tc, q, w, bias, offs, out):
             )
         sgn = held.tile([P, K], F32, name="sgn")
         nc.vector.tensor_scalar(out=sgn[:], in0=bit[:], scalar1=2.0, scalar2=-1.0, op0=ALU.mult, op1=ALU.add)
-
-        spread = held.tile([P, CODES, P], F32, name="spread")
-        nc.vector.memset(spread[:, 0, :], 0.0)
-        nc.vector.memset(spread[0:CODES, 0, :], 1.0 / CODES)
+        walsh = held.tile([P, CODES], F32, name="walsh")
+        nc.vector.memset(walsh[:, 0:1], 1.0 / (2 * CODES))
         for i in range(K):
             n = 1 << i
             nc.vector.tensor_scalar(
-                out=spread[:, n : 2 * n, :], in0=spread[:, 0:n, :], scalar1=sgn[:, i : i + 1], scalar2=None,
-                op0=ALU.mult,
+                out=walsh[:, n : 2 * n], in0=walsh[:, 0:n], scalar1=sgn[:, i : i + 1], scalar2=None, op0=ALU.mult
             )
+        identity = held.tile([P, P], F32, name="identity")
+        make_identity(nc, identity[:])
 
         coef = held.tile([P, CODES, T], F32, name="coef")
-        for m in range(0, CODES, 2):
-            bank = psum.tile([P, 2, T], F32, name="bank")
-            for j in range(2):
-                nc.tensor.matmul(bank[:, j, :], spread[:, m + j, :], w_pad[:], start=True, stop=True)
-            nc.scalar.copy(coef[:, m : m + 2, :], bank[:])
+        for e in odd_first(CODES // 2):
+            for m in (2 * e + 1, 2 * e):
+                if m > 0:
+                    bank = psum.tile([P, T], F32, name="bank")
+                    nc.tensor.matmul(bank[:], walsh[:, m : m + 1].to_broadcast([P, P]), w_pad[:], start=True, stop=True)
+                    nc.scalar.copy(coef[:, m, :], bank[:])
+        total = psum_total.tile([P, T], F32, name="total")
+        for l in range(LEVELS):
+            nc.tensor.matmul(total[:], walsh[:, 0:1].to_broadcast([P, P]), w_pad[:], start=(l == 0), stop=False)
 
         value = [coef for l in range(LEVELS)]
         for i in range(K):
             n = CODES >> (i + 1)
             picks = offsets[:, i * (T // 16) : (i + 1) * (T // 16)]
+            after = [held.tile([P, n, T], F32, name=f"u{i + 1}_{l}") for l in range(LEVELS)]
+            for e in odd_first(n):
+                for l in range(LEVELS):
+                    nc.vector.tensor_tensor(
+                        after[l][:, e, :], window[l][:].indirect(picks), value[l][:, 2 * e + 1, :], ALU.mult
+                    )
             for l in range(LEVELS):
-                pairs = value[l][:].rearrange("p (e two) t -> p e two t", two=2)
-                after = held.tile([P, n, T], F32, name=f"u{i + 1}_{l}")
-                for e in range(n):
-                    nc.vector.tensor_tensor(after[:, e, :], window[l][:].indirect(picks), pairs[:, e, 1, :], ALU.mult)
-                nc.vector.tensor_tensor(after[:], after[:], pairs[:, :, 0, :], ALU.add)
-                value[l] = after
+                if n > 1:
+                    new = after[l][:].rearrange("p (h two) t -> p h two t", two=2)
+                    old = value[l][:].rearrange("p (h four) t -> p h four t", four=4)
+                    nc.gpsimd.tensor_tensor(new[:, :, 1, :], new[:, :, 1, :], old[:, :, 2, :], ALU.add)
+                    if n > 2:
+                        nc.gpsimd.tensor_tensor(new[:, 1:, 0, :], new[:, 1:, 0, :], old[:, 1:, 0, :], ALU.add)
+                    nc.tensor.matmul(
+                        total[:], identity[:], after[l][:, 0, :], start=False, stop=(n == 2 and l == LEVELS - 1)
+                    )
+            value = after
 
         both = held.tile([P, T], F32, name="both")
-        nc.vector.tensor_tensor(both[:], value[0][:, 0, :], value[1][:, 0, :], ALU.add)
+        nc.vector.tensor_tensor(both[:], value[0][:, 0, :], total[:], ALU.add)
+        nc.vector.tensor_tensor(both[:], both[:], value[1][:, 0, :], ALU.add)
         sums = held.tile([P, OUT], F32, name="sums")
         nc.vector.tensor_reduce(
             out=sums[:], in_=both[:].rearrange("p (o s) -> p o s", s=PER), axis=mybir.AxisListType.X, op=ALU.add

@@ -12,29 +12,44 @@ S = 2048
 T = 256
 K = 4
 CODES = 16
+HALF = CODES // 2
 OUT = 16
 PER = 16
 N = K * T
+COLS = T // 16
+WARM = 2
 
 FLOPS = 2 * (CODES - 1) * LEVELS * P * T
 
 
-def odd_first(n):
-    return list(range(1, n, 2)) + list(range(0, n, 2))
+def which_input(step, h):
+    return (step + h) % (K - 1)
+
+
+def monomial(low, h):
+    return HALF * h + sum([((low >> step) & 1) << which_input(step, h) for step in range(K - 1)])
 
 
 def tile_linearlut_kernel(tc, q, w, bias, offs, out):
     nc = tc.nc
     with (
         tc.tile_pool(name="held", bufs=1) as held,
-        tc.psum_pool(name="psum", bufs=6) as psum,
-        tc.psum_pool(name="psum_total", bufs=1) as psum_total,
+        tc.psum_pool(name="psum", bufs=4) as psum,
+        tc.psum_pool(name="chains", bufs=1) as chains,
     ):
+        part = held.tile([P, 1], I32, name="part")
+        nc.gpsimd.iota(part[:], pattern=[[0, 1]], base=0, channel_multiplier=1)
+        zeros = held.tile([P, T], F32, name="zeros")
+        nc.gpsimd.memset(zeros[:], 0.0)
+        for k in range(WARM):
+            bank = psum.tile([P, T], F32, name="bank")
+            nc.tensor.matmul(bank[:], zeros[:, 0:P], zeros[:], start=True, stop=True)
+
         w_pad = held.tile([P, T], F32, name="w_pad")
         for rep in range(2):
-            nc.scalar.dma_start(w_pad[rep * CODES : (rep + 1) * CODES, :], w)
-        nc.any.memset(w_pad[32:64, :], 0.0)
-        nc.any.memset(w_pad[64:128, :], 0.0)
+            nc.sync.dma_start(w_pad[rep * CODES : (rep + 1) * CODES, :], w)
+        nc.gpsimd.memset(w_pad[32:64, :], 0.0)
+        nc.gpsimd.memset(w_pad[64:128, :], 0.0)
         offsets = held.tile([P, N // 16], U16, name="offsets")
         nc.sync.dma_start(offsets[:], offs)
         window = []
@@ -43,10 +58,8 @@ def tile_linearlut_kernel(tc, q, w, bias, offs, out):
             nc.sync.dma_start(q_l[:], q[l * P : (l + 1) * P, :])
             window.append(q_l)
         bias_all = held.tile([P, OUT], F32, name="bias_all")
-        nc.scalar.dma_start(bias_all[:], bias.to_broadcast([P, OUT]))
+        nc.sync.dma_start(bias_all[:], bias.to_broadcast([P, OUT]))
 
-        part = held.tile([P, 1], I32, name="part")
-        nc.gpsimd.iota(part[:], pattern=[[0, 1]], base=0, channel_multiplier=1)
         bit = held.tile([P, K], I32, name="bit")
         for i in range(K):
             nc.vector.tensor_scalar(
@@ -65,45 +78,65 @@ def tile_linearlut_kernel(tc, q, w, bias, offs, out):
         identity = held.tile([P, P], F32, name="identity")
         make_identity(nc, identity[:])
 
-        coef = held.tile([P, CODES, T], F32, name="coef")
-        for e in odd_first(CODES // 2):
-            for m in (2 * e + 1, 2 * e):
-                if m > 0:
-                    bank = psum.tile([P, T], F32, name="bank")
-                    nc.tensor.matmul(bank[:], walsh[:, m : m + 1].to_broadcast([P, P]), w_pad[:], start=True, stop=True)
-                    nc.scalar.copy(coef[:, m, :], bank[:])
-        total = psum_total.tile([P, T], F32, name="total")
+        def spread(low, h):
+            m = monomial(low, h)
+            return walsh[:, m : m + 1].to_broadcast([P, P])
+
+        coef = held.tile([P, HALF, 2, T], F32, name="coef")
+        for low in list(range(1, HALF, 2)) + list(range(2, HALF, 2)):
+            for h in range(2):
+                bank = psum.tile([P, T], F32, name="bank")
+                nc.tensor.matmul(bank[:], spread(low, h), w_pad[:], start=True, stop=True)
+                nc.scalar.copy(coef[:, low, h, :], bank[:])
+        total = chains.tile([P, T], F32, name="total")
+        top = [chains.tile([P, T], F32, name=f"top{l}") for l in range(LEVELS)]
         for l in range(LEVELS):
-            nc.tensor.matmul(total[:], walsh[:, 0:1].to_broadcast([P, P]), w_pad[:], start=(l == 0), stop=False)
+            nc.tensor.matmul(total[:], spread(0, 0), w_pad[:], start=(l == 0), stop=False)
+            nc.tensor.matmul(top[l][:], spread(0, 1), w_pad[:], start=True, stop=False)
+        bias_share = held.tile([P, OUT, PER], F32, name="bias_share")
+        nc.scalar.mul(out=bias_share[:], in_=bias_all[:].unsqueeze(2).to_broadcast([P, OUT, PER]), mul=1.0 / PER)
+        nc.tensor.matmul(total[:], identity[:], bias_share[:].rearrange("p o s -> p (o s)"), start=False, stop=False)
+
+        def look_up(l, first, count):
+            return window[l][:].indirect(offsets[:, first * COLS : (first + count) * COLS])
 
         value = [coef for l in range(LEVELS)]
-        for i in range(K):
-            n = CODES >> (i + 1)
-            picks = offsets[:, i * (T // 16) : (i + 1) * (T // 16)]
-            after = [held.tile([P, n, T], F32, name=f"u{i + 1}_{l}") for l in range(LEVELS)]
-            for e in odd_first(n):
-                for l in range(LEVELS):
-                    nc.vector.tensor_tensor(
-                        after[l][:, e, :], window[l][:].indirect(picks), value[l][:, 2 * e + 1, :], ALU.mult
-                    )
+        for step in range(K - 1):
+            n = HALF >> (step + 1)
+            after = [held.tile([P, n, 2, T], F32, name=f"u{step + 1}_{l}") for l in range(LEVELS)]
             for l in range(LEVELS):
+                new = after[l][:].rearrange("p j h t -> p j (h t)")
+                old = value[l][:].rearrange("p j h t -> p j (h t)")
+                for j in range(n):
+                    if which_input(step, 1) == which_input(step, 0) + 1:
+                        nc.vector.tensor_tensor(
+                            new[:, j, :], look_up(l, which_input(step, 0), 2), old[:, 2 * j + 1, :], ALU.mult
+                        )
+                    else:
+                        for h in range(2):
+                            nc.vector.tensor_tensor(
+                                after[l][:, j, h, :], look_up(l, which_input(step, h), 1),
+                                value[l][:, 2 * j + 1, h, :], ALU.mult,
+                            )
+            for l in range(LEVELS):
+                nc.tensor.matmul(
+                    total[:], identity[:], after[l][:, 0, 0, :], start=False, stop=(n == 1 and l == LEVELS - 1)
+                )
                 if n > 1:
-                    new = after[l][:].rearrange("p (h two) t -> p h two t", two=2)
-                    old = value[l][:].rearrange("p (h four) t -> p h four t", four=4)
-                    nc.gpsimd.tensor_tensor(new[:, :, 1, :], new[:, :, 1, :], old[:, :, 2, :], ALU.add)
-                    if n > 2:
-                        nc.gpsimd.tensor_tensor(new[:, 1:, 0, :], new[:, 1:, 0, :], old[:, 1:, 0, :], ALU.add)
-                    nc.tensor.matmul(
-                        total[:], identity[:], after[l][:, 0, :], start=False, stop=(n == 2 and l == LEVELS - 1)
-                    )
+                    nc.tensor.matmul(top[l][:], identity[:], after[l][:, 0, 1, :], start=False, stop=(n == 2))
+                    new = after[l][:].rearrange("p j h t -> p j (h t)")
+                    old = value[l][:].rearrange("p (j two) h t -> p j two (h t)", two=2)
+                    nc.vector.tensor_tensor(new[:, 1:, :], new[:, 1:, :], old[:, 1:, 0, :], ALU.add)
+                else:
+                    nc.vector.tensor_tensor(after[l][:, 0, 1, :], after[l][:, 0, 1, :], top[l][:], ALU.add)
             value = after
 
-        both = held.tile([P, T], F32, name="both")
-        nc.vector.tensor_tensor(both[:], value[0][:, 0, :], total[:], ALU.add)
-        nc.vector.tensor_tensor(both[:], both[:], value[1][:, 0, :], ALU.add)
+        last = held.tile([P, LEVELS, T], F32, name="last")
+        for l in range(LEVELS):
+            nc.vector.tensor_tensor(last[:, l, :], look_up(l, K - 1, 1), value[l][:, 0, 1, :], ALU.mult)
+        nc.vector.tensor_tensor(last[:, 0, :], last[:, 0, :], total[:], ALU.add)
         sums = held.tile([P, OUT], F32, name="sums")
         nc.vector.tensor_reduce(
-            out=sums[:], in_=both[:].rearrange("p (o s) -> p o s", s=PER), axis=mybir.AxisListType.X, op=ALU.add
+            out=sums[:], in_=last[:].rearrange("p l (o s) -> p o l s", s=PER), axis=mybir.AxisListType.XY, op=ALU.add
         )
-        nc.vector.tensor_tensor(sums[:], sums[:], bias_all[:], ALU.add)
         nc.sync.dma_start(out, sums[:])

@@ -50,6 +50,8 @@ def tile_linearlut_kernel(tc, q, w, bias, offs, out):
             nc.sync.dma_start(w_pad[rep * CODES : (rep + 1) * CODES, :], w)
         nc.gpsimd.memset(w_pad[32:64, :], 0.0)
         nc.gpsimd.memset(w_pad[64:128, :], 0.0)
+        bias_all = held.tile([P, OUT], F32, name="bias_all")
+        nc.sync.dma_start(bias_all[:], bias.to_broadcast([P, OUT]))
         offsets = held.tile([P, N // 16], U16, name="offsets")
         nc.sync.dma_start(offsets[:], offs)
         window = []
@@ -57,8 +59,6 @@ def tile_linearlut_kernel(tc, q, w, bias, offs, out):
             q_l = held.tile([P, S], F32, name=f"q{l}")
             nc.sync.dma_start(q_l[:], q[l * P : (l + 1) * P, :])
             window.append(q_l)
-        bias_all = held.tile([P, OUT], F32, name="bias_all")
-        nc.sync.dma_start(bias_all[:], bias.to_broadcast([P, OUT]))
 
         bit = held.tile([P, K], I32, name="bit")
         for i in range(K):

@@ -101,39 +101,39 @@ def tile_linearlut_kernel(tc, q, w, bias, offs, out):
             return window[l][:].indirect(offsets[:, first * COLS : (first + count) * COLS])
 
         value = [coef for l in range(LEVELS)]
-        for step in range(K - 1):
+        for step in range(2):
             n = HALF >> (step + 1)
             after = [held.tile([P, n, 2, T], F32, name=f"u{step + 1}_{l}") for l in range(LEVELS)]
             for l in range(LEVELS):
                 new = after[l][:].rearrange("p j h t -> p j (h t)")
                 old = value[l][:].rearrange("p j h t -> p j (h t)")
                 for j in range(n):
-                    if which_input(step, 1) == which_input(step, 0) + 1:
-                        nc.vector.tensor_tensor(
-                            new[:, j, :], look_up(l, which_input(step, 0), 2), old[:, 2 * j + 1, :], ALU.mult
-                        )
-                    else:
-                        for h in range(2):
-                            nc.vector.tensor_tensor(
-                                after[l][:, j, h, :], look_up(l, which_input(step, h), 1),
-                                value[l][:, 2 * j + 1, h, :], ALU.mult,
-                            )
+                    nc.vector.tensor_tensor(
+                        new[:, j, :], look_up(l, which_input(step, 0), 2), old[:, 2 * j + 1, :], ALU.mult
+                    )
             for l in range(LEVELS):
-                nc.tensor.matmul(
-                    total[:], identity[:], after[l][:, 0, 0, :], start=False, stop=(n == 1 and l == LEVELS - 1)
-                )
-                if n > 1:
-                    nc.tensor.matmul(top[l][:], identity[:], after[l][:, 0, 1, :], start=False, stop=(n == 2))
-                    new = after[l][:].rearrange("p j h t -> p j (h t)")
-                    old = value[l][:].rearrange("p (j two) h t -> p j two (h t)", two=2)
-                    nc.vector.tensor_tensor(new[:, 1:, :], new[:, 1:, :], old[:, 1:, 0, :], ALU.add)
-                else:
-                    nc.vector.tensor_tensor(after[l][:, 0, 1, :], after[l][:, 0, 1, :], top[l][:], ALU.add)
+                nc.tensor.matmul(total[:], identity[:], after[l][:, 0, 0, :], start=False, stop=False)
+                nc.tensor.matmul(top[l][:], identity[:], after[l][:, 0, 1, :], start=False, stop=False)
+                new = after[l][:].rearrange("p j h t -> p j (h t)")
+                old = value[l][:].rearrange("p (j two) h t -> p j two (h t)", two=2)
+                nc.vector.tensor_tensor(new[:, 1:, :], new[:, 1:, :], old[:, 1:, 0, :], ALU.add)
             value = after
+
+        third = [held.tile([P, 2, T], F32, name=f"u3_{l}") for l in range(LEVELS)]
+        for h in (1, 0):
+            for l in range(LEVELS):
+                nc.vector.tensor_tensor(
+                    third[l][:, h, :], look_up(l, which_input(2, h), 1), value[l][:, 1, h, :], ALU.mult
+                )
+                if h == 1:
+                    nc.tensor.matmul(top[l][:], identity[:], third[l][:, h, :], start=False, stop=True)
+                    nc.scalar.copy(third[l][:, h, :], top[l][:])
+                else:
+                    nc.tensor.matmul(total[:], identity[:], third[l][:, h, :], start=False, stop=(l == LEVELS - 1))
 
         last = held.tile([P, LEVELS, T], F32, name="last")
         for l in range(LEVELS):
-            nc.vector.tensor_tensor(last[:, l, :], look_up(l, K - 1, 1), value[l][:, 0, 1, :], ALU.mult)
+            nc.vector.tensor_tensor(last[:, l, :], look_up(l, K - 1, 1), third[l][:, 1, :], ALU.mult)
         nc.vector.tensor_tensor(last[:, 0, :], last[:, 0, :], total[:], ALU.add)
         sums = held.tile([P, OUT], F32, name="sums")
         nc.vector.tensor_reduce(

@@ -17,7 +17,7 @@ OUT = 16
 PER = 16
 N = K * T
 COLS = T // 16
-WARM = 2
+WARM = 3
 
 FLOPS = 2 * (CODES - 1) * LEVELS * P * T
 
@@ -37,13 +37,13 @@ def tile_linearlut_kernel(tc, q, w, bias, offs, out):
         tc.psum_pool(name="psum", bufs=4) as psum,
         tc.psum_pool(name="chains", bufs=1) as chains,
     ):
-        part = held.tile([P, 1], I32, name="part")
-        nc.gpsimd.iota(part[:], pattern=[[0, 1]], base=0, channel_multiplier=1)
-        zeros = held.tile([P, T], F32, name="zeros")
-        nc.gpsimd.memset(zeros[:], 0.0)
+        count = held.tile([P, T], F32, name="count")
+        nc.gpsimd.iota(count[:], pattern=[[1, T]], base=0, channel_multiplier=1, allow_small_or_imprecise_dtypes=True)
         for k in range(WARM):
             bank = psum.tile([P, T], F32, name="bank")
-            nc.tensor.matmul(bank[:], zeros[:, 0:P], zeros[:], start=True, stop=True)
+            nc.tensor.matmul(bank[:], count[:, 0:P], count[:], start=True, stop=True)
+        part = held.tile([P, 1], I32, name="part")
+        nc.gpsimd.iota(part[:], pattern=[[0, 1]], base=0, channel_multiplier=1)
 
         w_pad = held.tile([P, T], F32, name="w_pad")
         for rep in range(2):

@@ -17,7 +17,7 @@ OUT = 16
 PER = 16
 N = K * T
 COLS = T // 16
-WARM = 3
+WARM = 2
 
 FLOPS = 2 * (CODES - 1) * LEVELS * P * T
 
@@ -37,13 +37,13 @@ def tile_linearlut_kernel(tc, q, w, bias, offs, out):
         tc.psum_pool(name="psum", bufs=4) as psum,
         tc.psum_pool(name="chains", bufs=1) as chains,
     ):
-        count = held.tile([P, T], F32, name="count")
-        nc.gpsimd.iota(count[:], pattern=[[1, T]], base=0, channel_multiplier=1, allow_small_or_imprecise_dtypes=True)
-        for k in range(WARM):
-            bank = psum.tile([P, T], F32, name="bank")
-            nc.tensor.matmul(bank[:], count[:, 0:P], count[:], start=True, stop=True)
         part = held.tile([P, 1], I32, name="part")
         nc.gpsimd.iota(part[:], pattern=[[0, 1]], base=0, channel_multiplier=1)
+        zeros = held.tile([P, T], F32, name="zeros")
+        nc.gpsimd.memset(zeros[:], 0.0)
+        for k in range(WARM):
+            bank = psum.tile([P, T], F32, name="bank")
+            nc.tensor.matmul(bank[:], zeros[:, 0:P], zeros[:], start=True, stop=True)
 
         w_pad = held.tile([P, T], F32, name="w_pad")
         for rep in range(2):
@@ -68,19 +68,18 @@ def tile_linearlut_kernel(tc, q, w, bias, offs, out):
             )
         sgn = held.tile([P, K], F32, name="sgn")
         nc.vector.tensor_scalar(out=sgn[:], in0=bit[:], scalar1=2.0, scalar2=-1.0, op0=ALU.mult, op1=ALU.add)
-        walsh = held.tile([P, CODES], F32, name="walsh")
-        nc.vector.memset(walsh[:, 0:1], 1.0 / (2 * CODES))
+        walsh = held.tile([P, CODES, P], F32, name="walsh")
+        nc.vector.memset(walsh[:, 0, :], 1.0 / (2 * CODES))
         for i in range(K):
             n = 1 << i
             nc.vector.tensor_scalar(
-                out=walsh[:, n : 2 * n], in0=walsh[:, 0:n], scalar1=sgn[:, i : i + 1], scalar2=None, op0=ALU.mult
+                out=walsh[:, n : 2 * n, :], in0=walsh[:, 0:n, :], scalar1=sgn[:, i : i + 1], scalar2=None, op0=ALU.mult
             )
         identity = held.tile([P, P], F32, name="identity")
         make_identity(nc, identity[:])
 
         def spread(low, h):
-            m = monomial(low, h)
-            return walsh[:, m : m + 1].to_broadcast([P, P])
+            return walsh[:, monomial(low, h), :]
 
         coef = held.tile([P, HALF, 2, T], F32, name="coef")
         for low in list(range(1, HALF, 2)) + list(range(2, HALF, 2)):

@@ -50,8 +50,6 @@ def tile_linearlut_kernel(tc, q, w, bias, offs, out):
             nc.sync.dma_start(w_pad[rep * CODES : (rep + 1) * CODES, :], w)
         nc.gpsimd.memset(w_pad[32:64, :], 0.0)
         nc.gpsimd.memset(w_pad[64:128, :], 0.0)
-        bias_all = held.tile([P, OUT], F32, name="bias_all")
-        nc.sync.dma_start(bias_all[:], bias.to_broadcast([P, OUT]))
         offsets = held.tile([P, N // 16], U16, name="offsets")
         nc.sync.dma_start(offsets[:], offs)
         window = []
@@ -59,6 +57,8 @@ def tile_linearlut_kernel(tc, q, w, bias, offs, out):
             q_l = held.tile([P, S], F32, name=f"q{l}")
             nc.sync.dma_start(q_l[:], q[l * P : (l + 1) * P, :])
             window.append(q_l)
+        bias_all = held.tile([P, OUT], F32, name="bias_all")
+        nc.sync.dma_start(bias_all[:], bias.to_broadcast([P, OUT]))
 
         bit = held.tile([P, K], I32, name="bit")
         for i in range(K):
@@ -68,18 +68,19 @@ def tile_linearlut_kernel(tc, q, w, bias, offs, out):
             )
         sgn = held.tile([P, K], F32, name="sgn")
         nc.vector.tensor_scalar(out=sgn[:], in0=bit[:], scalar1=2.0, scalar2=-1.0, op0=ALU.mult, op1=ALU.add)
-        walsh = held.tile([P, CODES, P], F32, name="walsh")
-        nc.vector.memset(walsh[:, 0, :], 1.0 / (2 * CODES))
+        walsh = held.tile([P, CODES], F32, name="walsh")
+        nc.vector.memset(walsh[:, 0:1], 1.0 / (2 * CODES))
         for i in range(K):
             n = 1 << i
             nc.vector.tensor_scalar(
-                out=walsh[:, n : 2 * n, :], in0=walsh[:, 0:n, :], scalar1=sgn[:, i : i + 1], scalar2=None, op0=ALU.mult
+                out=walsh[:, n : 2 * n], in0=walsh[:, 0:n], scalar1=sgn[:, i : i + 1], scalar2=None, op0=ALU.mult
             )
         identity = held.tile([P, P], F32, name="identity")
         make_identity(nc, identity[:])
 
         def spread(low, h):
-            return walsh[:, monomial(low, h), :]
+            m = monomial(low, h)
+            return walsh[:, m : m + 1].to_broadcast([P, P])
 
         coef = held.tile([P, HALF, 2, T], F32, name="coef")
         for low in list(range(1, HALF, 2)) + list(range(2, HALF, 2)):
@@ -92,9 +93,6 @@ def tile_linearlut_kernel(tc, q, w, bias, offs, out):
         for l in range(LEVELS):
             nc.tensor.matmul(total[:], spread(0, 0), w_pad[:], start=(l == 0), stop=False)
             nc.tensor.matmul(top[l][:], spread(0, 1), w_pad[:], start=True, stop=False)
-        bias_share = held.tile([P, OUT, PER], F32, name="bias_share")
-        nc.scalar.mul(out=bias_share[:], in_=bias_all[:].unsqueeze(2).to_broadcast([P, OUT, PER]), mul=1.0 / PER)
-        nc.tensor.matmul(total[:], identity[:], bias_share[:].rearrange("p o s -> p (o s)"), start=False, stop=False)
 
         def look_up(l, first, count):
             return window[l][:].indirect(offsets[:, first * COLS : (first + count) * COLS])
@@ -138,4 +136,5 @@ def tile_linearlut_kernel(tc, q, w, bias, offs, out):
         nc.vector.tensor_reduce(
             out=sums[:], in_=last[:].rearrange("p l (o s) -> p o l s", s=PER), axis=mybir.AxisListType.XY, op=ALU.add
         )
+        nc.vector.tensor_tensor(sums[:], sums[:], bias_all[:], ALU.add)
         nc.sync.dma_start(out, sums[:])

@@ -2,6 +2,7 @@ import concourse.mybir as mybir
 from concourse.masks import make_identity
 
 F32 = mybir.dt.float32
+BF16 = mybir.dt.bfloat16
 I32 = mybir.dt.int32
 U16 = mybir.dt.uint16
 ALU = mybir.AluOpType
@@ -17,6 +18,7 @@ OUT = 16
 PER = 16
 N = K * T
 COLS = T // 16
+PARTS = 3
 WARM = 2
 
 FLOPS = 2 * (CODES - 1) * LEVELS * P * T
@@ -34,7 +36,7 @@ def tile_linearlut_kernel(tc, q, w, bias, offs, out):
     nc = tc.nc
     with (
         tc.tile_pool(name="held", bufs=1) as held,
-        tc.psum_pool(name="psum", bufs=4) as psum,
+        tc.psum_pool(name="turns", bufs=3) as turns,
         tc.psum_pool(name="chains", bufs=1) as chains,
     ):
         part = held.tile([P, 1], I32, name="part")
@@ -42,14 +44,13 @@ def tile_linearlut_kernel(tc, q, w, bias, offs, out):
         zeros = held.tile([P, T], F32, name="zeros")
         nc.gpsimd.memset(zeros[:], 0.0)
         for k in range(WARM):
-            bank = psum.tile([P, T], F32, name="bank")
-            nc.tensor.matmul(bank[:], zeros[:, 0:P], zeros[:], start=True, stop=True)
+            bank = turns.tile([P, 2, T], F32, name="bank")
+            nc.tensor.matmul(bank[:, 0, :], zeros[:, 0:P], zeros[:], start=True, stop=True)
 
-        w_pad = held.tile([P, T], F32, name="w_pad")
-        for rep in range(2):
-            nc.sync.dma_start(w_pad[rep * CODES : (rep + 1) * CODES, :], w)
-        nc.gpsimd.memset(w_pad[32:64, :], 0.0)
-        nc.gpsimd.memset(w_pad[64:128, :], 0.0)
+        w_rows = held.tile([P, T], F32, name="w_rows")
+        for k in range(2 * PARTS):
+            nc.sync.dma_start(w_rows[k * CODES : (k + 1) * CODES, :], w)
+        nc.gpsimd.memset(w_rows[96:128, :], 0.0)
         offsets = held.tile([P, N // 16], U16, name="offsets")
         nc.sync.dma_start(offsets[:], offs)
         window = []
@@ -68,69 +69,118 @@ def tile_linearlut_kernel(tc, q, w, bias, offs, out):
             )
         sgn = held.tile([P, K], F32, name="sgn")
         nc.vector.tensor_scalar(out=sgn[:], in0=bit[:], scalar1=2.0, scalar2=-1.0, op0=ALU.mult, op1=ALU.add)
-        walsh = held.tile([P, CODES], F32, name="walsh")
+        walsh = held.tile([P, CODES], BF16, name="walsh")
         nc.vector.memset(walsh[:, 0:1], 1.0 / (2 * CODES))
         for i in range(K):
             n = 1 << i
             nc.vector.tensor_scalar(
                 out=walsh[:, n : 2 * n], in0=walsh[:, 0:n], scalar1=sgn[:, i : i + 1], scalar2=None, op0=ALU.mult
             )
+        peel = held.tile([P, PARTS - 1], F32, name="peel")
+        for k in range(PARTS - 1):
+            nc.vector.tensor_scalar(
+                out=peel[:, k : k + 1], in0=part[:], scalar1=32 * (k + 1), scalar2=-1.0, op0=ALU.is_ge, op1=ALU.mult
+            )
         identity = held.tile([P, P], F32, name="identity")
         make_identity(nc, identity[:])
 
-        def spread(low, h):
-            m = monomial(low, h)
-            return walsh[:, m : m + 1].to_broadcast([P, P])
+        def cut(tile_ap):
+            return tile_ap.bitcast(BF16).rearrange("p (t two) -> p t two", two=2)[:, :, 1]
 
-        coef = held.tile([P, HALF, 2, T], F32, name="coef")
-        for low in list(range(1, HALF, 2)) + list(range(2, HALF, 2)):
-            for h in range(2):
-                bank = psum.tile([P, T], F32, name="bank")
-                nc.tensor.matmul(bank[:], spread(low, h), w_pad[:], start=True, stop=True)
-                nc.scalar.copy(coef[:, low, h, :], bank[:])
-        total = chains.tile([P, T], F32, name="total")
-        top = [chains.tile([P, T], F32, name=f"top{l}") for l in range(LEVELS)]
-        for l in range(LEVELS):
-            nc.tensor.matmul(total[:], spread(0, 0), w_pad[:], start=(l == 0), stop=False)
-            nc.tensor.matmul(top[l][:], spread(0, 1), w_pad[:], start=True, stop=False)
+        rest = w_rows
+        for k in range(PARTS - 1):
+            left = held.tile([P, T], F32, name=f"left{k}")
+            nc.vector.scalar_tensor_tensor(
+                out=left[:], in0=cut(rest[:]), scalar=peel[:, k : k + 1], in1=rest[:], op0=ALU.mult, op1=ALU.add
+            )
+            rest = left
+        w_parts = cut(rest[:])
+
+        def coefficient(acc, low, h, start, stop):
+            m = monomial(low, h)
+            nc.tensor.matmul(acc, walsh[:, m : m + 1].to_broadcast([P, P]), w_parts, start=start, stop=stop)
+
+        def coefficients(acc, low):
+            coefficient(acc[:, 0, :], low, 0, True, False)
+            coefficient(acc[:, 1, :], low, 1, False, False)
+
+        def add(acc, product, start, stop):
+            nc.tensor.matmul(acc, identity[:], product, start=start, stop=stop)
+
+        def both(tile_ap):
+            return tile_ap.rearrange("p h t -> p (h t)")
 
         def look_up(l, first, count):
             return window[l][:].indirect(offsets[:, first * COLS : (first + count) * COLS])
 
-        value = [coef for l in range(LEVELS)]
-        for step in range(2):
-            n = HALF >> (step + 1)
-            after = [held.tile([P, n, 2, T], F32, name=f"u{step + 1}_{l}") for l in range(LEVELS)]
-            for l in range(LEVELS):
-                new = after[l][:].rearrange("p j h t -> p j (h t)")
-                old = value[l][:].rearrange("p j h t -> p j (h t)")
-                for j in range(n):
-                    nc.vector.tensor_tensor(
-                        new[:, j, :], look_up(l, which_input(step, 0), 2), old[:, 2 * j + 1, :], ALU.mult
-                    )
-            for l in range(LEVELS):
-                nc.tensor.matmul(total[:], identity[:], after[l][:, 0, 0, :], start=False, stop=False)
-                nc.tensor.matmul(top[l][:], identity[:], after[l][:, 0, 1, :], start=False, stop=False)
-                new = after[l][:].rearrange("p j h t -> p j (h t)")
-                old = value[l][:].rearrange("p (j two) h t -> p j two (h t)", two=2)
-                nc.vector.tensor_tensor(new[:, 1:, :], new[:, 1:, :], old[:, 1:, 0, :], ALU.add)
-            value = after
+        ORDER = (3, 1, 2, 0)
+        odd = held.tile([P, HALF // 2, 2, T], F32, name="odd")
+        for j in ORDER:
+            bank = turns.tile([P, 2, T], F32, name="bank")
+            for h in range(2):
+                coefficient(bank[:, h, :], 2 * j + 1, h, True, True)
+            nc.scalar.copy(odd[:, j, :, :], bank[:])
 
-        third = [held.tile([P, 2, T], F32, name=f"u3_{l}") for l in range(LEVELS)]
+        total = chains.tile([P, T], F32, name="total")
+        top = [chains.tile([P, T], F32, name=f"top{l}") for l in range(LEVELS)]
+        mid = [chains.tile([P, 2, T], F32, name=f"mid{l}") for l in range(LEVELS)]
+        for l in range(LEVELS):
+            coefficient(total[:], 0, 0, l == 0, False)
+            coefficient(top[l][:], 0, 1, True, False)
+            coefficients(mid[l], 4)
+        short = [(l, j) for l in range(LEVELS) for j in (3, 1)]
+        banks = {}
+
+        def open_bank(n):
+            if n < len(short):
+                banks[short[n]] = turns.tile([P, 2, T], F32, name="bank")
+                coefficients(banks[short[n]], 2 * short[n][1])
+
+        for n in range(3):
+            open_bank(n)
+
+        first = [held.tile([P, HALF // 2, 2, T], F32, name=f"first{l}") for l in range(LEVELS)]
+        u1 = [held.tile([P, 2, 2, T], F32, name=f"u1_{l}") for l in range(LEVELS)]
+        for l in range(LEVELS):
+            for j in ORDER:
+                nc.vector.tensor_tensor(both(first[l][:, j, :, :]), look_up(l, 0, 2), both(odd[:, j, :, :]), ALU.mult)
+                if j % 2 == 1:
+                    bank = banks[(l, j)]
+                    add(both(bank[:]), both(first[l][:, j, :, :]), False, True)
+                    nc.scalar.copy(u1[l][:, j // 2, :, :], bank[:])
+                    open_bank(short.index((l, j)) + 3)
+                elif j == 2:
+                    add(both(mid[l][:]), both(first[l][:, j, :, :]), False, False)
+                else:
+                    add(total[:], first[l][:, j, 0, :], False, False)
+                    add(top[l][:], first[l][:, j, 1, :], False, False)
+
+        second = [held.tile([P, 2, 2, T], F32, name=f"second{l}") for l in range(LEVELS)]
+        u2 = [held.tile([P, 2, T], F32, name=f"u2_{l}") for l in range(LEVELS)]
+        for j in (1, 0):
+            for l in range(LEVELS):
+                nc.vector.tensor_tensor(both(second[l][:, j, :, :]), look_up(l, 1, 2), both(u1[l][:, j, :, :]), ALU.mult)
+                if j == 1:
+                    add(both(mid[l][:]), both(second[l][:, j, :, :]), False, True)
+                    nc.scalar.copy(u2[l][:], mid[l][:])
+                else:
+                    add(total[:], second[l][:, j, 0, :], False, False)
+                    add(top[l][:], second[l][:, j, 1, :], False, False)
+
+        third = [held.tile([P, 2, T], F32, name=f"third{l}") for l in range(LEVELS)]
+        u3 = [held.tile([P, T], F32, name=f"u3_{l}") for l in range(LEVELS)]
         for h in (1, 0):
             for l in range(LEVELS):
-                nc.vector.tensor_tensor(
-                    third[l][:, h, :], look_up(l, which_input(2, h), 1), value[l][:, 1, h, :], ALU.mult
-                )
+                nc.vector.tensor_tensor(third[l][:, h, :], look_up(l, which_input(2, h), 1), u2[l][:, h, :], ALU.mult)
                 if h == 1:
-                    nc.tensor.matmul(top[l][:], identity[:], third[l][:, h, :], start=False, stop=True)
-                    nc.scalar.copy(third[l][:, h, :], top[l][:])
+                    add(top[l][:], third[l][:, h, :], False, True)
+                    nc.scalar.copy(u3[l][:], top[l][:])
                 else:
-                    nc.tensor.matmul(total[:], identity[:], third[l][:, h, :], start=False, stop=(l == LEVELS - 1))
+                    add(total[:], third[l][:, h, :], False, l == LEVELS - 1)
 
         last = held.tile([P, LEVELS, T], F32, name="last")
         for l in range(LEVELS):
-            nc.vector.tensor_tensor(last[:, l, :], look_up(l, K - 1, 1), third[l][:, 1, :], ALU.mult)
+            nc.vector.tensor_tensor(last[:, l, :], look_up(l, K - 1, 1), u3[l][:], ALU.mult)
         nc.vector.tensor_tensor(last[:, 0, :], last[:, 0, :], total[:], ALU.add)
         sums = held.tile([P, OUT], F32, name="sums")
         nc.vector.tensor_reduce(

@@ -48,9 +48,9 @@ def tile_linearlut_kernel(tc, q, w, bias, offs, out):
             nc.tensor.matmul(bank[:, 0, :], zeros[:, 0:P], zeros[:], start=True, stop=True)
 
         w_rows = held.tile([P, T], F32, name="w_rows")
-        for k in range(2 * PARTS):
-            nc.sync.dma_start(w_rows[k * CODES : (k + 1) * CODES, :], w)
-        nc.gpsimd.memset(w_rows[96:128, :], 0.0)
+        for k in range(PARTS + 1):
+            (nc.sync if k % 2 == 0 else nc.scalar).dma_start(w_rows[k * CODES : (k + 1) * CODES, :], w)
+        nc.gpsimd.memset(w_rows[64:128, :], 0.0)
         offsets = held.tile([P, N // 16], U16, name="offsets")
         nc.sync.dma_start(offsets[:], offs)
         window = []
@@ -70,7 +70,9 @@ def tile_linearlut_kernel(tc, q, w, bias, offs, out):
         sgn = held.tile([P, K], F32, name="sgn")
         nc.vector.tensor_scalar(out=sgn[:], in0=bit[:], scalar1=2.0, scalar2=-1.0, op0=ALU.mult, op1=ALU.add)
         walsh = held.tile([P, CODES], BF16, name="walsh")
-        nc.vector.memset(walsh[:, 0:1], 1.0 / (2 * CODES))
+        nc.vector.tensor_scalar(
+            out=walsh[:, 0:1], in0=part[:], scalar1=PARTS * CODES, scalar2=1.0 / CODES, op0=ALU.is_lt, op1=ALU.mult
+        )
         for i in range(K):
             n = 1 << i
             nc.vector.tensor_scalar(
@@ -79,7 +81,7 @@ def tile_linearlut_kernel(tc, q, w, bias, offs, out):
         peel = held.tile([P, PARTS - 1], F32, name="peel")
         for k in range(PARTS - 1):
             nc.vector.tensor_scalar(
-                out=peel[:, k : k + 1], in0=part[:], scalar1=32 * (k + 1), scalar2=-1.0, op0=ALU.is_ge, op1=ALU.mult
+                out=peel[:, k : k + 1], in0=part[:], scalar1=CODES * (k + 1), scalar2=-1.0, op0=ALU.is_ge, op1=ALU.mult
             )
         identity = held.tile([P, P], F32, name="identity")
         make_identity(nc, identity[:])
@@ -164,27 +166,27 @@ def tile_linearlut_kernel(tc, q, w, bias, offs, out):
                     add(both(mid[l][:]), both(second[l][:, j, :, :]), False, True)
                     nc.scalar.copy(u2[l][:], mid[l][:])
                 else:
-                    add(total[:], second[l][:, j, 0, :], False, False)
                     add(top[l][:], second[l][:, j, 1, :], False, False)
 
-        third = [held.tile([P, 2, T], F32, name=f"third{l}") for l in range(LEVELS)]
+        third = [held.tile([P, T], F32, name=f"third{l}") for l in range(LEVELS)]
         u3 = [held.tile([P, T], F32, name=f"u3_{l}") for l in range(LEVELS)]
+        tail = held.tile([P, 2 * LEVELS, T], F32, name="tail")
         for h in (1, 0):
             for l in range(LEVELS):
-                nc.vector.tensor_tensor(third[l][:, h, :], look_up(l, which_input(2, h), 1), u2[l][:, h, :], ALU.mult)
+                product = third[l][:] if h == 1 else tail[:, l, :]
+                nc.vector.tensor_tensor(product, look_up(l, which_input(2, h), 1), u2[l][:, h, :], ALU.mult)
                 if h == 1:
-                    add(top[l][:], third[l][:, h, :], False, True)
+                    add(top[l][:], product, False, True)
                     nc.scalar.copy(u3[l][:], top[l][:])
                 else:
-                    add(total[:], third[l][:, h, :], False, l == LEVELS - 1)
+                    add(total[:], second[l][:, 0, 0, :], False, l == LEVELS - 1)
 
-        last = held.tile([P, LEVELS, T], F32, name="last")
         for l in range(LEVELS):
-            nc.vector.tensor_tensor(last[:, l, :], look_up(l, K - 1, 1), u3[l][:], ALU.mult)
-        nc.vector.tensor_tensor(last[:, 0, :], last[:, 0, :], total[:], ALU.add)
+            nc.vector.tensor_tensor(tail[:, LEVELS + l, :], look_up(l, K - 1, 1), u3[l][:], ALU.mult)
+        nc.vector.tensor_tensor(tail[:, 0, :], tail[:, 0, :], total[:], ALU.add)
         sums = held.tile([P, OUT], F32, name="sums")
         nc.vector.tensor_reduce(
-            out=sums[:], in_=last[:].rearrange("p l (o s) -> p o l s", s=PER), axis=mybir.AxisListType.XY, op=ALU.add
+            out=sums[:], in_=tail[:].rearrange("p n (o s) -> p o n s", s=PER), axis=mybir.AxisListType.XY, op=ALU.add
         )
         nc.vector.tensor_tensor(sums[:], sums[:], bias_all[:], ALU.add)
         nc.sync.dma_start(out, sums[:])

@@ -181,6 +181,9 @@ def tile_linearlut_kernel(tc, q, w, bias, offs, out):
                 else:
                     add(total[:], second[l][:, 0, 0, :], False, l == LEVELS - 1)
 
+        leaders = tail[:, 0, :].rearrange("p (o s) -> p o s", s=PER)[:, :, 0]
+        nc.vector.tensor_tensor(leaders, leaders, bias_all[:], ALU.add)
+
         for l in range(LEVELS):
             nc.vector.tensor_tensor(tail[:, LEVELS + l, :], look_up(l, K - 1, 1), u3[l][:], ALU.mult)
         nc.vector.tensor_tensor(tail[:, 0, :], tail[:, 0, :], total[:], ALU.add)
@@ -188,5 +191,4 @@ def tile_linearlut_kernel(tc, q, w, bias, offs, out):
         nc.vector.tensor_reduce(
             out=sums[:], in_=tail[:].rearrange("p n (o s) -> p o n s", s=PER), axis=mybir.AxisListType.XY, op=ALU.add
         )
-        nc.vector.tensor_tensor(sums[:], sums[:], bias_all[:], ALU.add)
         nc.sync.dma_start(out, sums[:])

@@ -69,7 +69,7 @@ def tile_linearlut_kernel(tc, q, w, bias, offs, out):
             )
         sgn = held.tile([P, K], F32, name="sgn")
         nc.vector.tensor_scalar(out=sgn[:], in0=bit[:], scalar1=2.0, scalar2=-1.0, op0=ALU.mult, op1=ALU.add)
-        walsh = held.tile([P, CODES], BF16, name="walsh")
+        walsh = held.tile([P, CODES + 1], BF16, name="walsh")
         nc.vector.tensor_scalar(
             out=walsh[:, 0:1], in0=part[:], scalar1=PARTS * CODES, scalar2=1.0 / CODES, op0=ALU.is_lt, op1=ALU.mult
         )
@@ -78,6 +78,9 @@ def tile_linearlut_kernel(tc, q, w, bias, offs, out):
             nc.vector.tensor_scalar(
                 out=walsh[:, n : 2 * n], in0=walsh[:, 0:n], scalar1=sgn[:, i : i + 1], scalar2=None, op0=ALU.mult
             )
+        nc.vector.tensor_scalar(
+            out=walsh[:, CODES : CODES + 1], in0=walsh[:, 0:1], scalar1=float(LEVELS), scalar2=None, op0=ALU.mult
+        )
         peel = held.tile([P, PARTS - 1], F32, name="peel")
         for k in range(PARTS - 1):
             nc.vector.tensor_scalar(
@@ -126,8 +129,8 @@ def tile_linearlut_kernel(tc, q, w, bias, offs, out):
         total = chains.tile([P, T], F32, name="total")
         top = [chains.tile([P, T], F32, name=f"top{l}") for l in range(LEVELS)]
         mid = [chains.tile([P, 2, T], F32, name=f"mid{l}") for l in range(LEVELS)]
+        nc.tensor.matmul(total[:], walsh[:, CODES : CODES + 1].to_broadcast([P, P]), w_parts, start=True, stop=False)
         for l in range(LEVELS):
-            coefficient(total[:], 0, 0, l == 0, False)
             coefficient(top[l][:], 0, 1, True, False)
             coefficients(mid[l], 4)
         short = [(l, j) for l in range(LEVELS) for j in (3, 1)]

@@ -13,7 +13,6 @@ S = 2048
 T = 256
 K = 4
 CODES = 16
-HALF = CODES // 2
 OUT = 16
 PER = 16
 N = K * T
@@ -24,40 +23,47 @@ WARM = 2
 FLOPS = 2 * (CODES - 1) * LEVELS * P * T
 
 
-def which_input(step, h):
-    return (step + h) % (K - 1)
+def monomial(*inputs):
+    return sum([1 << (i % K) for i in inputs])
 
 
-def monomial(low, h):
-    return HALF * h + sum([((low >> step) & 1) << which_input(step, h) for step in range(K - 1)])
+ALL = monomial(0, 1, 2, 3)
+ALL_BY = 1
+TRIPLE = [monomial(i - 1, i, i + 1) for i in range(K)]
+OPPOSITE = [monomial(i, i + 2) for i in range(2)]
+NEIGHBOUR = [monomial(i - 1, i) for i in range(K)]
+SINGLE = [monomial(i) for i in range(K)]
+INNER = (ALL_BY + 2) % K
 
 
 def tile_linearlut_kernel(tc, q, w, bias, offs, out):
     nc = tc.nc
     with (
         tc.tile_pool(name="held", bufs=1) as held,
-        tc.psum_pool(name="turns", bufs=3) as turns,
-        tc.psum_pool(name="chains", bufs=1) as chains,
+        tc.tile_pool(name="wide", bufs=2) as wide,
+        tc.psum_pool(name="banks", bufs=8) as banks,
     ):
+        def new_bank():
+            bank = banks.tile([P, 2, T], F32, name="bank")
+            return bank
+
         part = held.tile([P, 1], I32, name="part")
         nc.gpsimd.iota(part[:], pattern=[[0, 1]], base=0, channel_multiplier=1)
         zeros = held.tile([P, T], F32, name="zeros")
         nc.gpsimd.memset(zeros[:], 0.0)
         for k in range(WARM):
-            bank = turns.tile([P, 2, T], F32, name="bank")
-            nc.tensor.matmul(bank[:, 0, :], zeros[:, 0:P], zeros[:], start=True, stop=True)
+            warm = new_bank()
+            nc.tensor.matmul(warm[:, 0, :], zeros[:, 0:P], zeros[:], start=True, stop=True)
 
         w_rows = held.tile([P, T], F32, name="w_rows")
         for k in range(PARTS + 1):
             (nc.sync if k % 2 == 0 else nc.scalar).dma_start(w_rows[k * CODES : (k + 1) * CODES, :], w)
         nc.gpsimd.memset(w_rows[64:128, :], 0.0)
+        window = [held.tile([P, S], F32, name=f"q{l}") for l in range(LEVELS)]
+        nc.sync.dma_start(window[0][:], q[0:P, :])
         offsets = held.tile([P, N // 16], U16, name="offsets")
         nc.sync.dma_start(offsets[:], offs)
-        window = []
-        for l in range(LEVELS):
-            q_l = held.tile([P, S], F32, name=f"q{l}")
-            nc.sync.dma_start(q_l[:], q[l * P : (l + 1) * P, :])
-            window.append(q_l)
+        nc.sync.dma_start(window[1][:], q[P : 2 * P, :])
         bias_all = held.tile([P, OUT], F32, name="bias_all")
         nc.sync.dma_start(bias_all[:], bias.to_broadcast([P, OUT]))
 
@@ -101,97 +107,131 @@ def tile_linearlut_kernel(tc, q, w, bias, offs, out):
             rest = left
         w_parts = cut(rest[:])
 
-        def coefficient(acc, low, h, start, stop):
-            m = monomial(low, h)
+        def coefficient(acc, m, start, stop):
             nc.tensor.matmul(acc, walsh[:, m : m + 1].to_broadcast([P, P]), w_parts, start=start, stop=stop)
 
-        def coefficients(acc, low):
-            coefficient(acc[:, 0, :], low, 0, True, False)
-            coefficient(acc[:, 1, :], low, 1, False, False)
+        def staged(*products):
+            bank = new_bank()
+            for h, m in enumerate(products):
+                coefficient(bank[:, h, :], m, True, True)
+            return bank
 
-        def add(acc, product, start, stop):
-            nc.tensor.matmul(acc, identity[:], product, start=start, stop=stop)
+        def opened(*products):
+            bank = new_bank()
+            for h, m in enumerate(products):
+                coefficient(bank[:, h, :], m, h == 0, False)
+            return bank
 
-        def both(tile_ap):
-            return tile_ap.rearrange("p h t -> p (h t)")
+        def add(acc, product, stop):
+            nc.tensor.matmul(acc, identity[:], product, start=False, stop=stop)
 
-        def look_up(l, first, count):
-            return window[l][:].indirect(offsets[:, first * COLS : (first + count) * COLS])
+        def run(tile_ap):
+            return tile_ap.rearrange("p n t -> p (n t)")
 
-        ORDER = (3, 1, 2, 0)
-        odd = held.tile([P, HALF // 2, 2, T], F32, name="odd")
-        for j in ORDER:
-            bank = turns.tile([P, 2, T], F32, name="bank")
-            for h in range(2):
-                coefficient(bank[:, h, :], 2 * j + 1, h, True, True)
-            nc.scalar.copy(odd[:, j, :, :], bank[:])
+        def look_up(l, first, count, multiplicand, product):
+            picked = window[l][:].indirect(offsets[:, first * COLS : (first + count) * COLS])
+            nc.vector.tensor_tensor(product, picked, multiplicand, ALU.mult)
 
-        total = chains.tile([P, T], F32, name="total")
-        top = [chains.tile([P, T], F32, name=f"top{l}") for l in range(LEVELS)]
-        mid = [chains.tile([P, 2, T], F32, name=f"mid{l}") for l in range(LEVELS)]
-        nc.tensor.matmul(total[:], walsh[:, CODES : CODES + 1].to_broadcast([P, P]), w_parts, start=True, stop=False)
-        for l in range(LEVELS):
-            coefficient(top[l][:], 0, 1, True, False)
-            coefficients(mid[l], 4)
-        short = [(l, j) for l in range(LEVELS) for j in (3, 1)]
-        banks = {}
+        all_m = [held.tile([P, T], F32, name=f"all_m{l}") for l in range(LEVELS)]
+        neighbour_m = held.tile([P, K, T], F32, name="neighbour_m")
+        triple_m = held.tile([P, INNER, T], F32, name="triple_m")
+        inner_m = [held.tile([P, T], F32, name=f"inner_m{l}") for l in range(LEVELS)]
+        opposite_m = [held.tile([P, 2, T], F32, name=f"opposite_m{l}") for l in range(LEVELS)]
+        single_m = [held.tile([P, K, T], F32, name=f"single_m{l}") for l in range(LEVELS)]
+        all_p = [held.tile([P, T], F32, name=f"all_p{l}") for l in range(LEVELS)]
+        neighbour_p = [held.tile([P, K, T], F32, name="neighbour_p")]
+        triple_p = []
+        opposite_p = [held.tile([P, 2, T], F32, name=f"opposite_p{l}") for l in range(LEVELS)]
+        terms = [held.tile([P, K, T], F32, name=f"terms{l}") for l in range(LEVELS)]
 
-        def open_bank(n):
-            if n < len(short):
-                banks[short[n]] = turns.tile([P, 2, T], F32, name="bank")
-                coefficients(banks[short[n]], 2 * short[n][1])
+        bank_all = staged(ALL)
+        nc.scalar.copy(all_m[0][:], bank_all[:, 0, :])
+        for i in (0, 2):
+            pair = staged(NEIGHBOUR[i], NEIGHBOUR[i + 1])
+            nc.scalar.copy(neighbour_m[:, i : i + 2, :], pair[:])
+        nc.scalar.copy(all_m[1][:], bank_all[:, 0, :])
+        inner = [opened(TRIPLE[INNER])]
+        pair = staged(TRIPLE[0], TRIPLE[1])
+        nc.scalar.copy(triple_m[:, 0:2, :], pair[:])
+        third = staged(TRIPLE[2])
+        nc.scalar.copy(triple_m[:, 2, :], third[:, 0, :])
 
-        for n in range(3):
-            open_bank(n)
+        def take_all(l):
+            look_up(l, ALL_BY, 1, all_m[l][:], all_p[l][:])
+            add(inner[l][:, 0, :], all_p[l][:], True)
+            nc.scalar.copy(inner_m[l][:], inner[l][:, 0, :])
 
-        first = [held.tile([P, HALF // 2, 2, T], F32, name=f"first{l}") for l in range(LEVELS)]
-        u1 = [held.tile([P, 2, 2, T], F32, name=f"u1_{l}") for l in range(LEVELS)]
-        for l in range(LEVELS):
-            for j in ORDER:
-                nc.vector.tensor_tensor(both(first[l][:, j, :, :]), look_up(l, 0, 2), both(odd[:, j, :, :]), ALU.mult)
-                if j % 2 == 1:
-                    bank = banks[(l, j)]
-                    add(both(bank[:]), both(first[l][:, j, :, :]), False, True)
-                    nc.scalar.copy(u1[l][:, j // 2, :, :], bank[:])
-                    open_bank(short.index((l, j)) + 3)
-                elif j == 2:
-                    add(both(mid[l][:]), both(first[l][:, j, :, :]), False, False)
-                else:
-                    add(total[:], first[l][:, j, 0, :], False, False)
-                    add(top[l][:], first[l][:, j, 1, :], False, False)
+        def take_triples(l):
+            wide_p = wide.tile([P, K, T], F32, name="wide_p")
+            triple_p.append(wide_p)
+            look_up(l, 0, INNER, run(triple_m[:]), run(triple_p[l][:, 0:INNER, :]))
+            add(run(opposite[l][:]), run(triple_p[l][:, 0:2, :]), False)
+            add(opposite[l][:, 0, :], triple_p[l][:, 2, :], False)
 
-        second = [held.tile([P, 2, 2, T], F32, name=f"second{l}") for l in range(LEVELS)]
-        u2 = [held.tile([P, 2, T], F32, name=f"u2_{l}") for l in range(LEVELS)]
-        for j in (1, 0):
-            for l in range(LEVELS):
-                nc.vector.tensor_tensor(both(second[l][:, j, :, :]), look_up(l, 1, 2), both(u1[l][:, j, :, :]), ALU.mult)
-                if j == 1:
-                    add(both(mid[l][:]), both(second[l][:, j, :, :]), False, True)
-                    nc.scalar.copy(u2[l][:], mid[l][:])
-                else:
-                    add(top[l][:], second[l][:, j, 1, :], False, False)
+        def take_inner(l):
+            look_up(l, INNER, 1, inner_m[l][:], triple_p[l][:, INNER, :])
+            add(opposite[l][:, 1, :], triple_p[l][:, INNER, :], True)
+            for i in range(2):
+                nc.scalar.copy(opposite_m[l][:, i, :], opposite[l][:, 1 - i, :])
 
-        third = [held.tile([P, T], F32, name=f"third{l}") for l in range(LEVELS)]
-        u3 = [held.tile([P, T], F32, name=f"u3_{l}") for l in range(LEVELS)]
-        tail = held.tile([P, 2 * LEVELS, T], F32, name="tail")
-        for h in (1, 0):
-            for l in range(LEVELS):
-                product = third[l][:] if h == 1 else tail[:, l, :]
-                nc.vector.tensor_tensor(product, look_up(l, which_input(2, h), 1), u2[l][:, h, :], ALU.mult)
-                if h == 1:
-                    add(top[l][:], product, False, True)
-                    nc.scalar.copy(u3[l][:], top[l][:])
-                else:
-                    add(total[:], second[l][:, 0, 0, :], False, l == LEVELS - 1)
+        def take_neighbours(l):
+            if l > 0:
+                wide_p = wide.tile([P, K, T], F32, name="wide_p")
+                neighbour_p.append(wide_p)
+            for i in (0, 2):
+                look_up(l, i, 2, run(neighbour_m[:, i : i + 2, :]), run(neighbour_p[l][:, i : i + 2, :]))
+            for i in range(K):
+                left = (i - 1) % K
+                add(single[l][left // 2][:, left % 2, :], neighbour_p[l][:, i, :], i == 2)
+            nc.scalar.copy(single_m[l][:, 0:2, :], single[l][0][:])
 
-        leaders = tail[:, 0, :].rearrange("p (o s) -> p o s", s=PER)[:, :, 0]
-        nc.vector.tensor_tensor(leaders, leaders, bias_all[:], ALU.add)
+        def take_opposite(l, width):
+            for i in range(0, 2, width):
+                places = slice(i, i + width)
+                look_up(l, i, width, run(opposite_m[l][:, places, :]), run(opposite_p[l][:, places, :]))
+                add(run(single[l][1][:, places, :]), run(opposite_p[l][:, places, :]), i + width == 2)
+            for i in range(0, 2, width):
+                nc.scalar.copy(single_m[l][:, 2 + i : 2 + i + width, :], single[l][1][:, i : i + width, :])
 
-        for l in range(LEVELS):
-            nc.vector.tensor_tensor(tail[:, LEVELS + l, :], look_up(l, K - 1, 1), u3[l][:], ALU.mult)
-        nc.vector.tensor_tensor(tail[:, 0, :], tail[:, 0, :], total[:], ALU.add)
+        def take_singles(l, first):
+            places = slice(first, first + 2)
+            look_up(l, first, 2, run(single_m[l][:, places, :]), run(terms[l][:, places, :]))
+
+        def add_term(l, i, stop):
+            add(total[:, 0, :], terms[l][:, i, :], stop)
+
+        take_all(0)
+        single = [[opened(SINGLE[0], SINGLE[1]), opened(SINGLE[2], SINGLE[3])]]
+        inner.append(opened(TRIPLE[INNER]))
+        single.append([opened(SINGLE[0], SINGLE[1]), opened(SINGLE[2], SINGLE[3])])
+        opposite = [opened(OPPOSITE[1], OPPOSITE[0]) for l in range(LEVELS)]
+        take_neighbours(0)
+        take_all(1)
+        take_triples(0)
+        take_inner(0)
+        take_triples(1)
+        take_inner(1)
+        total = new_bank()
+        coefficient(total[:, 0, :], CODES, True, False)
+        take_singles(0, 0)
+        add_term(0, 0, False)
+        take_neighbours(1)
+        take_opposite(0, 2)
+        take_opposite(1, 2)
+        add_term(0, 1, False)
+        take_singles(1, 0)
+        take_singles(0, 2)
+        for l, i in ((1, 0), (1, 1), (0, 2), (0, 3)):
+            add_term(l, i, (l, i) == (0, 3))
+        take_singles(1, 2)
+
+        def by_feature(sums, tables):
+            nc.vector.tensor_reduce(out=sums, in_=tables, axis=mybir.AxisListType.XY, op=ALU.add)
+
+        last = held.tile([P, OUT], F32, name="last")
         sums = held.tile([P, OUT], F32, name="sums")
-        nc.vector.tensor_reduce(
-            out=sums[:], in_=tail[:].rearrange("p n (o s) -> p o n s", s=PER), axis=mybir.AxisListType.XY, op=ALU.add
-        )
+        by_feature(last[:], terms[1][:, 2:4, :].rearrange("p n (o s) -> p o n s", s=PER))
+        nc.vector.tensor_tensor(last[:], last[:], bias_all[:], ALU.add)
+        by_feature(sums[:], total[:, 0:1, :].rearrange("p n (o s) -> p o n s", s=PER))
+        nc.vector.tensor_tensor(sums[:], sums[:], last[:], ALU.add)
         nc.sync.dma_start(out, sums[:])

@@ -18,6 +18,7 @@ PER = 16
 N = K * T
 COLS = T // 16
 PARTS = 3
+ONE_16TH = 0x3D800000
 WARM = 2
 
 FLOPS = 2 * (CODES - 1) * LEVELS * P * T
@@ -49,16 +50,17 @@ def tile_linearlut_kernel(tc, q, w, bias, offs, out):
 
         part = held.tile([P, 1], I32, name="part")
         nc.gpsimd.iota(part[:], pattern=[[0, 1]], base=0, channel_multiplier=1)
+        column = held.tile([P, CODES], I32, name="column")
+        nc.gpsimd.iota(column[:], pattern=[[1, CODES]], base=0, channel_multiplier=0)
         zeros = held.tile([P, T], F32, name="zeros")
         nc.gpsimd.memset(zeros[:], 0.0)
         for k in range(WARM):
             warm = new_bank()
             nc.tensor.matmul(warm[:, 0, :], zeros[:, 0:P], zeros[:], start=True, stop=True)
 
-        w_rows = held.tile([P, T], F32, name="w_rows")
-        for k in range(PARTS + 1):
-            (nc.sync if k % 2 == 0 else nc.scalar).dma_start(w_rows[k * CODES : (k + 1) * CODES, :], w)
-        nc.gpsimd.memset(w_rows[64:128, :], 0.0)
+        w_rows = held.tile([PARTS * CODES, T], F32, name="w_rows")
+        for k in range(PARTS):
+            (nc.scalar if k == 1 else nc.sync).dma_start(w_rows[k * CODES : (k + 1) * CODES, :], w)
         window = [held.tile([P, S], F32, name=f"q{l}") for l in range(LEVELS)]
         nc.sync.dma_start(window[0][:], q[0:P, :])
         offsets = held.tile([P, N // 16], U16, name="offsets")
@@ -67,44 +69,44 @@ def tile_linearlut_kernel(tc, q, w, bias, offs, out):
         bias_all = held.tile([P, OUT], F32, name="bias_all")
         nc.sync.dma_start(bias_all[:], bias.to_broadcast([P, OUT]))
 
-        bit = held.tile([P, K], I32, name="bit")
-        for i in range(K):
-            nc.vector.tensor_scalar(
-                out=bit[:, i : i + 1], in0=part[:], scalar1=i, scalar2=1,
-                op0=ALU.logical_shift_right, op1=ALU.bitwise_and,
-            )
-        sgn = held.tile([P, K], F32, name="sgn")
-        nc.vector.tensor_scalar(out=sgn[:], in0=bit[:], scalar1=2.0, scalar2=-1.0, op0=ALU.mult, op1=ALU.add)
-        walsh = held.tile([P, CODES + 1], BF16, name="walsh")
-        nc.vector.tensor_scalar(
-            out=walsh[:, 0:1], in0=part[:], scalar1=PARTS * CODES, scalar2=1.0 / CODES, op0=ALU.is_lt, op1=ALU.mult
-        )
-        for i in range(K):
-            n = 1 << i
-            nc.vector.tensor_scalar(
-                out=walsh[:, n : 2 * n], in0=walsh[:, 0:n], scalar1=sgn[:, i : i + 1], scalar2=None, op0=ALU.mult
-            )
-        nc.vector.tensor_scalar(
-            out=walsh[:, CODES : CODES + 1], in0=walsh[:, 0:1], scalar1=float(LEVELS), scalar2=None, op0=ALU.mult
-        )
-        peel = held.tile([P, PARTS - 1], F32, name="peel")
+        peel = []
         for k in range(PARTS - 1):
-            nc.vector.tensor_scalar(
-                out=peel[:, k : k + 1], in0=part[:], scalar1=CODES * (k + 1), scalar2=-1.0, op0=ALU.is_ge, op1=ALU.mult
+            behind = held.tile([PARTS * CODES, 1], F32, name=f"behind{k}")
+            nc.gpsimd.memset(behind[:], -1.0)
+            nc.gpsimd.memset(behind[0 : (k + 1) * CODES, :], 0.0)
+            peel.append(behind)
+        bits = held.tile([P, CODES], I32, name="bits")
+        nc.vector.scalar_tensor_tensor(
+            out=bits[:], in0=part[:].to_broadcast([P, CODES]), scalar=CODES - 1, in1=column[:],
+            op0=ALU.bitwise_xor, op1=ALU.bitwise_and,
+        )
+        for shift in (2, 1):
+            folded = held.tile([P, CODES], I32, name=f"folded{shift}")
+            nc.vector.scalar_tensor_tensor(
+                out=folded[:], in0=bits[:], scalar=shift, in1=bits[:], op0=ALU.logical_shift_right, op1=ALU.bitwise_xor
             )
+            bits = folded
+        signed = held.tile([P, CODES], I32, name="signed")
+        nc.vector.tensor_scalar(
+            out=signed[:], in0=bits[:], scalar1=31, scalar2=ONE_16TH, op0=ALU.logical_shift_left, op1=ALU.bitwise_xor
+        )
         identity = held.tile([P, P], F32, name="identity")
         make_identity(nc, identity[:])
 
         def cut(tile_ap):
             return tile_ap.bitcast(BF16).rearrange("p (t two) -> p t two", two=2)[:, :, 1]
 
+        walsh = cut(signed[:])
+
+        left = [held.tile([rows, T], F32, name=f"left{rows}") for rows in (PARTS * CODES, P)]
+        nc.gpsimd.memset(left[-1][:], 0.0)
         rest = w_rows
         for k in range(PARTS - 1):
-            left = held.tile([P, T], F32, name=f"left{k}")
+            cut_off = left[k][0 : PARTS * CODES, :]
             nc.vector.scalar_tensor_tensor(
-                out=left[:], in0=cut(rest[:]), scalar=peel[:, k : k + 1], in1=rest[:], op0=ALU.mult, op1=ALU.add
+                out=cut_off, in0=cut(rest[:]), scalar=peel[k][:, 0:1], in1=rest[:], op0=ALU.mult, op1=ALU.add
             )
-            rest = left
+            rest = left[k]
         w_parts = cut(rest[:])
 
         def coefficient(acc, m, start, stop):
@@ -134,8 +136,8 @@ def tile_linearlut_kernel(tc, q, w, bias, offs, out):
 
         all_m = [held.tile([P, T], F32, name=f"all_m{l}") for l in range(LEVELS)]
         neighbour_m = held.tile([P, K, T], F32, name="neighbour_m")
-        triple_m = held.tile([P, INNER, T], F32, name="triple_m")
-        inner_m = [held.tile([P, T], F32, name=f"inner_m{l}") for l in range(LEVELS)]
+        triple_m = held.tile([P, K, T], F32, name="triple_m")
+        inner_m = [triple_m[:, INNER, :], held.tile([P, T], F32, name="inner_m")[:]]
         opposite_m = [held.tile([P, 2, T], F32, name=f"opposite_m{l}") for l in range(LEVELS)]
         single_m = [held.tile([P, K, T], F32, name=f"single_m{l}") for l in range(LEVELS)]
         all_p = [held.tile([P, T], F32, name=f"all_p{l}") for l in range(LEVELS)]
@@ -159,18 +161,25 @@ def tile_linearlut_kernel(tc, q, w, bias, offs, out):
         def take_all(l):
             look_up(l, ALL_BY, 1, all_m[l][:], all_p[l][:])
             add(inner[l][:, 0, :], all_p[l][:], True)
-            nc.scalar.copy(inner_m[l][:], inner[l][:, 0, :])
+            nc.scalar.copy(inner_m[l], inner[l][:, 0, :])
 
-        def take_triples(l):
+        def take_triples(l, count):
             wide_p = wide.tile([P, K, T], F32, name="wide_p")
             triple_p.append(wide_p)
-            look_up(l, 0, INNER, run(triple_m[:]), run(triple_p[l][:, 0:INNER, :]))
+            look_up(l, 0, count, run(triple_m[:, 0:count, :]), run(triple_p[l][:, 0:count, :]))
             add(run(opposite[l][:]), run(triple_p[l][:, 0:2, :]), False)
-            add(opposite[l][:, 0, :], triple_p[l][:, 2, :], False)
+            if count == K:
+                add(run(opposite[l][:]), run(triple_p[l][:, 2:4, :]), True)
+                copy_opposite(l)
+            else:
+                add(opposite[l][:, 0, :], triple_p[l][:, 2, :], False)
 
         def take_inner(l):
-            look_up(l, INNER, 1, inner_m[l][:], triple_p[l][:, INNER, :])
+            look_up(l, INNER, 1, inner_m[l], triple_p[l][:, INNER, :])
             add(opposite[l][:, 1, :], triple_p[l][:, INNER, :], True)
+            copy_opposite(l)
+
+        def copy_opposite(l):
             for i in range(2):
                 nc.scalar.copy(opposite_m[l][:, i, :], opposite[l][:, 1 - i, :])
 
@@ -207,12 +216,13 @@ def tile_linearlut_kernel(tc, q, w, bias, offs, out):
         opposite = [opened(OPPOSITE[1], OPPOSITE[0]) for l in range(LEVELS)]
         take_neighbours(0)
         take_all(1)
-        take_triples(0)
-        take_inner(0)
-        take_triples(1)
-        take_inner(1)
         total = new_bank()
-        coefficient(total[:, 0, :], CODES, True, False)
+        for l in range(LEVELS):
+            coefficient(total[:, 0, :], monomial(), l == 0, False)
+        add(total[:, 0, :].rearrange("p (o s) -> p o s", s=PER)[:, :, 0], bias_all[:], False)
+        take_triples(0, K)
+        take_triples(1, INNER)
+        take_inner(1)
         take_singles(0, 0)
         add_term(0, 0, False)
         take_neighbours(1)
@@ -231,7 +241,6 @@ def tile_linearlut_kernel(tc, q, w, bias, offs, out):
         last = held.tile([P, OUT], F32, name="last")
         sums = held.tile([P, OUT], F32, name="sums")
         by_feature(last[:], terms[1][:, 2:4, :].rearrange("p n (o s) -> p o n s", s=PER))
-        nc.vector.tensor_tensor(last[:], last[:], bias_all[:], ALU.add)
         by_feature(sums[:], total[:, 0:1, :].rearrange("p n (o s) -> p o n s", s=PER))
         nc.vector.tensor_tensor(sums[:], sums[:], last[:], ALU.add)
         nc.sync.dma_start(out, sums[:])

import concourse.mybir as mybir
from concourse.masks import make_identity

F32 = mybir.dt.float32
BF16 = mybir.dt.bfloat16
I32 = mybir.dt.int32
U16 = mybir.dt.uint16
ALU = mybir.AluOpType

P = 128
LEVELS = 2
S = 2048
T = 256
K = 4
CODES = 16
OUT = 16
PER = 16
N = K * T
COLS = T // 16
PARTS = 3
ONE_16TH = 0x3D800000
WARM = 2

FLOPS = 2 * (CODES - 1) * LEVELS * P * T


def monomial(*inputs):
    return sum([1 << (i % K) for i in inputs])


ALL = monomial(0, 1, 2, 3)
ALL_BY = 1
TRIPLE = [monomial(i - 1, i, i + 1) for i in range(K)]
OPPOSITE = [monomial(i, i + 2) for i in range(2)]
NEIGHBOUR = [monomial(i - 1, i) for i in range(K)]
SINGLE = [monomial(i) for i in range(K)]
INNER = (ALL_BY + 2) % K


def tile_linearlut_kernel(tc, q, w, bias, offs, out):
    nc = tc.nc
    with (
        tc.tile_pool(name="held", bufs=1) as held,
        tc.tile_pool(name="wide", bufs=2) as wide,
        tc.psum_pool(name="banks", bufs=8) as banks,
    ):
        def new_bank():
            bank = banks.tile([P, 2, T], F32, name="bank")
            return bank

        part = held.tile([P, 1], I32, name="part")
        nc.gpsimd.iota(part[:], pattern=[[0, 1]], base=0, channel_multiplier=1)
        column = held.tile([P, CODES], I32, name="column")
        nc.gpsimd.iota(column[:], pattern=[[1, CODES]], base=0, channel_multiplier=0)
        zeros = held.tile([P, T], F32, name="zeros")
        nc.gpsimd.memset(zeros[:], 0.0)
        for k in range(WARM):
            warm = new_bank()
            nc.tensor.matmul(warm[:, 0, :], zeros[:, 0:P], zeros[:], start=True, stop=True)

        w_rows = held.tile([PARTS * CODES, T], F32, name="w_rows")
        for k in range(PARTS):
            (nc.scalar if k == 1 else nc.sync).dma_start(w_rows[k * CODES : (k + 1) * CODES, :], w)
        window = [held.tile([P, S], F32, name=f"q{l}") for l in range(LEVELS)]
        nc.sync.dma_start(window[0][:], q[0:P, :])
        offsets = held.tile([P, N // 16], U16, name="offsets")
        nc.sync.dma_start(offsets[:], offs)
        nc.sync.dma_start(window[1][:], q[P : 2 * P, :])
        bias_all = held.tile([P, OUT], F32, name="bias_all")
        nc.sync.dma_start(bias_all[:], bias.to_broadcast([P, OUT]))

        peel = []
        for k in range(PARTS - 1):
            behind = held.tile([PARTS * CODES, 1], F32, name=f"behind{k}")
            nc.gpsimd.memset(behind[:], -1.0)
            nc.gpsimd.memset(behind[0 : (k + 1) * CODES, :], 0.0)
            peel.append(behind)
        bits = held.tile([P, CODES], I32, name="bits")
        nc.vector.scalar_tensor_tensor(
            out=bits[:], in0=part[:].to_broadcast([P, CODES]), scalar=CODES - 1, in1=column[:],
            op0=ALU.bitwise_xor, op1=ALU.bitwise_and,
        )
        for shift in (2, 1):
            folded = held.tile([P, CODES], I32, name=f"folded{shift}")
            nc.vector.scalar_tensor_tensor(
                out=folded[:], in0=bits[:], scalar=shift, in1=bits[:], op0=ALU.logical_shift_right, op1=ALU.bitwise_xor
            )
            bits = folded
        signed = held.tile([P, CODES], I32, name="signed")
        nc.vector.tensor_scalar(
            out=signed[:], in0=bits[:], scalar1=31, scalar2=ONE_16TH, op0=ALU.logical_shift_left, op1=ALU.bitwise_xor
        )
        identity = held.tile([P, P], F32, name="identity")
        make_identity(nc, identity[:])

        def cut(tile_ap):
            return tile_ap.bitcast(BF16).rearrange("p (t two) -> p t two", two=2)[:, :, 1]

        walsh = cut(signed[:])

        left = [held.tile([rows, T], F32, name=f"left{rows}") for rows in (PARTS * CODES, P)]
        nc.gpsimd.memset(left[-1][:], 0.0)
        rest = w_rows
        for k in range(PARTS - 1):
            cut_off = left[k][0 : PARTS * CODES, :]
            nc.vector.scalar_tensor_tensor(
                out=cut_off, in0=cut(rest[:]), scalar=peel[k][:, 0:1], in1=rest[:], op0=ALU.mult, op1=ALU.add
            )
            rest = left[k]
        w_parts = cut(rest[:])

        def coefficient(acc, m, start, stop):
            nc.tensor.matmul(acc, walsh[:, m : m + 1].to_broadcast([P, P]), w_parts, start=start, stop=stop)

        def staged(*products):
            bank = new_bank()
            for h, m in enumerate(products):
                coefficient(bank[:, h, :], m, True, True)
            return bank

        def opened(*products):
            bank = new_bank()
            for h, m in enumerate(products):
                coefficient(bank[:, h, :], m, h == 0, False)
            return bank

        def add(acc, product, stop):
            nc.tensor.matmul(acc, identity[:], product, start=False, stop=stop)

        def run(tile_ap):
            return tile_ap.rearrange("p n t -> p (n t)")

        def look_up(l, first, count, multiplicand, product):
            picked = window[l][:].indirect(offsets[:, first * COLS : (first + count) * COLS])
            nc.vector.tensor_tensor(product, picked, multiplicand, ALU.mult)

        all_m = [held.tile([P, T], F32, name=f"all_m{l}") for l in range(LEVELS)]
        neighbour_m = held.tile([P, K, T], F32, name="neighbour_m")
        triple_m = held.tile([P, K, T], F32, name="triple_m")
        inner_m = [triple_m[:, INNER, :], held.tile([P, T], F32, name="inner_m")[:]]
        opposite_m = [held.tile([P, 2, T], F32, name=f"opposite_m{l}") for l in range(LEVELS)]
        single_m = [held.tile([P, K, T], F32, name=f"single_m{l}") for l in range(LEVELS)]
        all_p = [held.tile([P, T], F32, name=f"all_p{l}") for l in range(LEVELS)]
        neighbour_p = [held.tile([P, K, T], F32, name="neighbour_p")]
        triple_p = []
        opposite_p = [held.tile([P, 2, T], F32, name=f"opposite_p{l}") for l in range(LEVELS)]
        terms = [held.tile([P, K, T], F32, name=f"terms{l}") for l in range(LEVELS)]

        bank_all = staged(ALL)
        nc.scalar.copy(all_m[0][:], bank_all[:, 0, :])
        for i in (0, 2):
            pair = staged(NEIGHBOUR[i], NEIGHBOUR[i + 1])
            nc.scalar.copy(neighbour_m[:, i : i + 2, :], pair[:])
        nc.scalar.copy(all_m[1][:], bank_all[:, 0, :])
        inner = [opened(TRIPLE[INNER])]
        pair = staged(TRIPLE[0], TRIPLE[1])
        nc.scalar.copy(triple_m[:, 0:2, :], pair[:])
        third = staged(TRIPLE[2])
        nc.scalar.copy(triple_m[:, 2, :], third[:, 0, :])

        def take_all(l):
            look_up(l, ALL_BY, 1, all_m[l][:], all_p[l][:])
            add(inner[l][:, 0, :], all_p[l][:], True)
            nc.scalar.copy(inner_m[l], inner[l][:, 0, :])

        def take_triples(l, count):
            wide_p = wide.tile([P, K, T], F32, name="wide_p")
            triple_p.append(wide_p)
            look_up(l, 0, count, run(triple_m[:, 0:count, :]), run(triple_p[l][:, 0:count, :]))
            add(run(opposite[l][:]), run(triple_p[l][:, 0:2, :]), False)
            if count == K:
                add(run(opposite[l][:]), run(triple_p[l][:, 2:4, :]), True)
                copy_opposite(l)
            else:
                add(opposite[l][:, 0, :], triple_p[l][:, 2, :], False)

        def take_inner(l):
            look_up(l, INNER, 1, inner_m[l], triple_p[l][:, INNER, :])
            add(opposite[l][:, 1, :], triple_p[l][:, INNER, :], True)
            copy_opposite(l)

        def copy_opposite(l):
            for i in range(2):
                nc.scalar.copy(opposite_m[l][:, i, :], opposite[l][:, 1 - i, :])

        def take_neighbours(l):
            if l > 0:
                wide_p = wide.tile([P, K, T], F32, name="wide_p")
                neighbour_p.append(wide_p)
            for i in (0, 2):
                look_up(l, i, 2, run(neighbour_m[:, i : i + 2, :]), run(neighbour_p[l][:, i : i + 2, :]))
            for i in range(K):
                left = (i - 1) % K
                add(single[l][left // 2][:, left % 2, :], neighbour_p[l][:, i, :], i == 2)
            nc.scalar.copy(single_m[l][:, 0:2, :], single[l][0][:])

        def take_opposite(l, width):
            for i in range(0, 2, width):
                places = slice(i, i + width)
                look_up(l, i, width, run(opposite_m[l][:, places, :]), run(opposite_p[l][:, places, :]))
                add(run(single[l][1][:, places, :]), run(opposite_p[l][:, places, :]), i + width == 2)
            for i in range(0, 2, width):
                nc.scalar.copy(single_m[l][:, 2 + i : 2 + i + width, :], single[l][1][:, i : i + width, :])

        def take_singles(l, first):
            places = slice(first, first + 2)
            look_up(l, first, 2, run(single_m[l][:, places, :]), run(terms[l][:, places, :]))

        def add_term(l, i, stop):
            add(total[:, 0, :], terms[l][:, i, :], stop)

        take_all(0)
        single = [[opened(SINGLE[0], SINGLE[1]), opened(SINGLE[2], SINGLE[3])]]
        inner.append(opened(TRIPLE[INNER]))
        single.append([opened(SINGLE[0], SINGLE[1]), opened(SINGLE[2], SINGLE[3])])
        opposite = [opened(OPPOSITE[1], OPPOSITE[0]) for l in range(LEVELS)]
        take_neighbours(0)
        take_all(1)
        total = new_bank()
        for l in range(LEVELS):
            coefficient(total[:, 0, :], monomial(), l == 0, False)
        add(total[:, 0, :].rearrange("p (o s) -> p o s", s=PER)[:, :, 0], bias_all[:], False)
        take_triples(0, K)
        take_triples(1, INNER)
        take_inner(1)
        take_singles(0, 0)
        add_term(0, 0, False)
        take_neighbours(1)
        take_opposite(0, 2)
        take_opposite(1, 2)
        add_term(0, 1, False)
        take_singles(1, 0)
        take_singles(0, 2)
        for l, i in ((1, 0), (1, 1), (0, 2), (0, 3)):
            add_term(l, i, (l, i) == (0, 3))
        take_singles(1, 2)

        def by_feature(sums, tables):
            nc.vector.tensor_reduce(out=sums, in_=tables, axis=mybir.AxisListType.XY, op=ALU.add)

        last = held.tile([P, OUT], F32, name="last")
        sums = held.tile([P, OUT], F32, name="sums")
        by_feature(last[:], terms[1][:, 2:4, :].rearrange("p n (o s) -> p o n s", s=PER))
        by_feature(sums[:], total[:, 0:1, :].rearrange("p n (o s) -> p o n s", s=PER))
        nc.vector.tensor_tensor(sums[:], sums[:], last[:], ALU.add)
        nc.sync.dma_start(out, sums[:])
